import numpy as np
import ml_dtypes

BF16 = ml_dtypes.bfloat16


def bf(x):
    return np.asarray(x, np.float32).astype(BF16)


def f32(x):
    return np.asarray(x, np.float32)


def f64(x):
    return np.asarray(x).astype(np.float64)


def striped(idx):
    return np.tile(idx.reshape(-1, 16).T, (8, 1))


D, S, M, N = 128, 512, 128, 1024


def sigmoid(v):
    return 1.0 / (1.0 + np.exp(-v))


def setup_inputs():
    return {"table": bf(np.random.standard_normal((D, S))), "w_src": bf(np.random.standard_normal((D, M)) / np.sqrt(D + D)), "w_dst": bf(np.random.standard_normal((D, M)) / np.sqrt(D + D)), "dst_f": bf(np.random.standard_normal((D, N))), "offs": striped(np.random.permutation(np.tile(np.arange(S), 2))[:N])}


def reference(table, w_src, w_dst, dst_f, offs):
    idx = offs[:16].T.reshape(-1)
    return sigmoid(f64(w_src).T @ f64(table)[:, idx] + f64(w_dst).T @ f64(dst_f))

@@ -1,0 +1,40 @@
+import concourse.mybir as mybir
+
+BF16, F32, U16 = mybir.dt.bfloat16, mybir.dt.float32, mybir.dt.uint16
+SIGMOID = mybir.ActivationFunctionType.Sigmoid
+
+P = 128
+NODES = 512
+EDGES = 1024
+PIECE = 512
+PER_COLUMN = 16
+
+FLOPS = 2 * (2 * P) * P * EDGES
+
+
+def tile_h_h_edgeapplymoudle_kernel(tc, table, w_src, w_dst, dst_f, offs, out):
+    nc = tc.nc
+    with (
+        tc.tile_pool(name="held", bufs=1) as held,
+        tc.psum_pool(name="psum", bufs=1) as psum,
+    ):
+        offsets = held.tile([P, EDGES // PER_COLUMN], U16, name="offsets")
+        nodes = held.tile([P, NODES], BF16, name="nodes")
+        src_weights = held.tile([P, P], BF16, name="src_weights")
+        dst_weights = held.tile([P, P], BF16, name="dst_weights")
+        dst_nodes = held.tile([P, EDGES], BF16, name="dst_nodes")
+        nc.sync.dma_start(offsets[:], offs)
+        nc.sync.dma_start(nodes[:], table)
+        nc.sync.dma_start(src_weights[:], w_src)
+        nc.sync.dma_start(dst_weights[:], w_dst)
+        nc.sync.dma_start(dst_nodes[:], dst_f)
+
+        for piece in range(EDGES // PIECE):
+            edges = slice(piece * PIECE, (piece + 1) * PIECE)
+            entries = slice(piece * PIECE // PER_COLUMN, (piece + 1) * PIECE // PER_COLUMN)
+            bank = psum.tile([P, PIECE], F32, name=f"bank{piece}")
+            gated = held.tile([P, PIECE], F32, name=f"gated{piece}")
+            nc.tensor.matmul(bank[:], src_weights[:], nodes[:].indirect(offsets[:, entries]), start=True, stop=False)
+            nc.tensor.matmul(bank[:], dst_weights[:], dst_nodes[:, edges], start=False, stop=True)
+            nc.scalar.activation(gated[:], bank[:], SIGMOID)
+            nc.sync.dma_start(out[:, edges], gated[:])

@@ -22,12 +22,13 @@ def tile_h_h_edgeapplymoudle_kernel(tc, table, w_src, w_dst, dst_f, offs, out):
         nodes = held.tile([P, NODES], BF16, name="nodes")
         src_weights = held.tile([P, P], BF16, name="src_weights")
         dst_weights = held.tile([P, P], BF16, name="dst_weights")
-        dst_nodes = held.tile([P, EDGES], BF16, name="dst_nodes")
+        dst_nodes = [held.tile([P, PIECE], BF16, name=f"dst_nodes{piece}") for piece in range(EDGES // PIECE)]
         nc.sync.dma_start(offsets[:], offs)
+        nc.scalar.dma_start(src_weights[:], w_src)
         nc.sync.dma_start(nodes[:], table)
-        nc.sync.dma_start(src_weights[:], w_src)
-        nc.sync.dma_start(dst_weights[:], w_dst)
-        nc.sync.dma_start(dst_nodes[:], dst_f)
+        nc.scalar.dma_start(dst_weights[:], w_dst)
+        nc.scalar.dma_start(dst_nodes[0][:], dst_f[:, 0:PIECE])
+        nc.sync.dma_start(dst_nodes[1][:], dst_f[:, PIECE : 2 * PIECE])
 
         for piece in range(EDGES // PIECE):
             edges = slice(piece * PIECE, (piece + 1) * PIECE)
@@ -35,6 +36,7 @@ def tile_h_h_edgeapplymoudle_kernel(tc, table, w_src, w_dst, dst_f, offs, out):
             bank = psum.tile([P, PIECE], F32, name=f"bank{piece}")
             gated = held.tile([P, PIECE], F32, name=f"gated{piece}")
             nc.tensor.matmul(bank[:], src_weights[:], nodes[:].indirect(offsets[:, entries]), start=True, stop=False)
-            nc.tensor.matmul(bank[:], dst_weights[:], dst_nodes[:, edges], start=False, stop=True)
+            nc.tensor.matmul(bank[:], dst_weights[:], dst_nodes[piece][:], start=False, stop=True)
             nc.scalar.activation(gated[:], bank[:], SIGMOID)
-            nc.sync.dma_start(out[:, edges], gated[:])
+            store_queue = nc.sync if piece == 0 else nc.scalar
+            store_queue.dma_start(out[:, edges], gated[:])

@@ -8,6 +8,7 @@ NODES = 512
 EDGES = 1024
 PIECE = 512
 PER_COLUMN = 16
+WARMING = 5
 
 FLOPS = 2 * (2 * P) * P * EDGES
 
@@ -29,6 +30,12 @@ def tile_h_h_edgeapplymoudle_kernel(tc, table, w_src, w_dst, dst_f, offs, out):
         nc.scalar.dma_start(dst_weights[:], w_dst)
         nc.scalar.dma_start(dst_nodes[0][:], dst_f[:, 0:PIECE])
         nc.sync.dma_start(dst_nodes[1][:], dst_f[:, PIECE : 2 * PIECE])
+
+        zeros = held.tile([P, PIECE], BF16, name="zeros")
+        unread = psum.tile([P, PIECE], F32, name="unread")
+        nc.vector.memset(zeros[:], 0.0)
+        for repeat in range(WARMING):
+            nc.tensor.matmul(unread[:], zeros[:, 0:P], zeros[:], start=True, stop=True)
 
         for piece in range(EDGES // PIECE):
             edges = slice(piece * PIECE, (piece + 1) * PIECE)

@@ -6,9 +6,8 @@ SIGMOID = mybir.ActivationFunctionType.Sigmoid
 P = 128
 NODES = 512
 EDGES = 1024
-PIECE = 512
+PIECE = 256
 PER_COLUMN = 16
-WARMING = 5
 
 FLOPS = 2 * (2 * P) * P * EDGES
 
@@ -23,19 +22,13 @@ def tile_h_h_edgeapplymoudle_kernel(tc, table, w_src, w_dst, dst_f, offs, out):
         nodes = held.tile([P, NODES], BF16, name="nodes")
         src_weights = held.tile([P, P], BF16, name="src_weights")
         dst_weights = held.tile([P, P], BF16, name="dst_weights")
-        dst_nodes = [held.tile([P, PIECE], BF16, name=f"dst_nodes{piece}") for piece in range(EDGES // PIECE)]
+        dst_nodes = held.tile([P, EDGES], BF16, name="dst_nodes")
         nc.sync.dma_start(offsets[:], offs)
         nc.scalar.dma_start(src_weights[:], w_src)
         nc.sync.dma_start(nodes[:], table)
         nc.scalar.dma_start(dst_weights[:], w_dst)
-        nc.scalar.dma_start(dst_nodes[0][:], dst_f[:, 0:PIECE])
-        nc.sync.dma_start(dst_nodes[1][:], dst_f[:, PIECE : 2 * PIECE])
-
-        zeros = held.tile([P, PIECE], BF16, name="zeros")
-        unread = psum.tile([P, PIECE], F32, name="unread")
-        nc.vector.memset(zeros[:], 0.0)
-        for repeat in range(WARMING):
-            nc.tensor.matmul(unread[:], zeros[:, 0:P], zeros[:], start=True, stop=True)
+        nc.scalar.dma_start(dst_nodes[:, 0 : EDGES // 2], dst_f[:, 0 : EDGES // 2])
+        nc.sync.dma_start(dst_nodes[:, EDGES // 2 : EDGES], dst_f[:, EDGES // 2 : EDGES])
 
         for piece in range(EDGES // PIECE):
             edges = slice(piece * PIECE, (piece + 1) * PIECE)
@@ -43,7 +36,7 @@ def tile_h_h_edgeapplymoudle_kernel(tc, table, w_src, w_dst, dst_f, offs, out):
             bank = psum.tile([P, PIECE], F32, name=f"bank{piece}")
             gated = held.tile([P, PIECE], F32, name=f"gated{piece}")
             nc.tensor.matmul(bank[:], src_weights[:], nodes[:].indirect(offsets[:, entries]), start=True, stop=False)
-            nc.tensor.matmul(bank[:], dst_weights[:], dst_nodes[piece][:], start=False, stop=True)
+            nc.tensor.matmul(bank[:], dst_weights[:], dst_nodes[:, edges], start=False, stop=True)
             nc.scalar.activation(gated[:], bank[:], SIGMOID)
-            store_queue = nc.sync if piece == 0 else nc.scalar
+            store_queue = nc.sync if piece < EDGES // PIECE - 1 else nc.scalar
             store_queue.dma_start(out[:, edges], gated[:])

@@ -6,10 +6,12 @@ SIGMOID = mybir.ActivationFunctionType.Sigmoid
 P = 128
 NODES = 512
 EDGES = 1024
-PIECE = 256
 PER_COLUMN = 16
 
 FLOPS = 2 * (2 * P) * P * EDGES
+
+PIECE = 256
+PIECES = EDGES // PIECE
 
 
 def tile_h_h_edgeapplymoudle_kernel(tc, table, w_src, w_dst, dst_f, offs, out):
@@ -22,21 +24,28 @@ def tile_h_h_edgeapplymoudle_kernel(tc, table, w_src, w_dst, dst_f, offs, out):
         nodes = held.tile([P, NODES], BF16, name="nodes")
         src_weights = held.tile([P, P], BF16, name="src_weights")
         dst_weights = held.tile([P, P], BF16, name="dst_weights")
-        dst_nodes = held.tile([P, EDGES], BF16, name="dst_nodes")
+        dst_nodes = [held.tile([P, PIECE], BF16, name=f"dst_nodes{piece}") for piece in range(PIECES)]
+        banks = [psum.tile([P, PIECE], F32, name=f"bank{piece}") for piece in range(PIECES)]
+
+        def edges_of(piece):
+            return slice(piece * PIECE, (piece + 1) * PIECE)
+
+        nc.scalar.dma_start(dst_weights[:], w_dst)
+        nc.sync.dma_start(dst_nodes[0][:], dst_f[:, edges_of(0)])
+        nc.scalar.dma_start(dst_nodes[1][:], dst_f[:, edges_of(1)])
+        nc.sync.dma_start(dst_nodes[2][:], dst_f[:, edges_of(2)])
+        nc.scalar.dma_start(dst_nodes[3][:], dst_f[:, edges_of(3)])
         nc.sync.dma_start(offsets[:], offs)
         nc.scalar.dma_start(src_weights[:], w_src)
         nc.sync.dma_start(nodes[:], table)
-        nc.scalar.dma_start(dst_weights[:], w_dst)
-        nc.scalar.dma_start(dst_nodes[:, 0 : EDGES // 2], dst_f[:, 0 : EDGES // 2])
-        nc.sync.dma_start(dst_nodes[:, EDGES // 2 : EDGES], dst_f[:, EDGES // 2 : EDGES])
 
-        for piece in range(EDGES // PIECE):
-            edges = slice(piece * PIECE, (piece + 1) * PIECE)
+        for piece in range(PIECES):
+            nc.tensor.matmul(banks[piece][:], dst_weights[:], dst_nodes[piece][:], start=True, stop=False)
+
+        for piece in range(PIECES):
             entries = slice(piece * PIECE // PER_COLUMN, (piece + 1) * PIECE // PER_COLUMN)
-            bank = psum.tile([P, PIECE], F32, name=f"bank{piece}")
             gated = held.tile([P, PIECE], F32, name=f"gated{piece}")
-            nc.tensor.matmul(bank[:], src_weights[:], nodes[:].indirect(offsets[:, entries]), start=True, stop=False)
-            nc.tensor.matmul(bank[:], dst_weights[:], dst_nodes[:, edges], start=False, stop=True)
-            nc.scalar.activation(gated[:], bank[:], SIGMOID)
-            store_queue = nc.sync if piece < EDGES // PIECE - 1 else nc.scalar
-            store_queue.dma_start(out[:, edges], gated[:])
+            nc.tensor.matmul(banks[piece][:], src_weights[:], nodes[:].indirect(offsets[:, entries]), start=False, stop=True)
+            nc.scalar.activation(gated[:], banks[piece][:], SIGMOID)
+            store_queue = nc.sync if piece < PIECES - 1 else nc.scalar
+            store_queue.dma_start(out[:, edges_of(piece)], gated[:])

@@ -30,13 +30,11 @@ def tile_h_h_edgeapplymoudle_kernel(tc, table, w_src, w_dst, dst_f, offs, out):
         def edges_of(piece):
             return slice(piece * PIECE, (piece + 1) * PIECE)
 
-        nc.scalar.dma_start(dst_weights[:], w_dst)
-        nc.sync.dma_start(dst_nodes[0][:], dst_f[:, edges_of(0)])
-        nc.scalar.dma_start(dst_nodes[1][:], dst_f[:, edges_of(1)])
-        nc.sync.dma_start(dst_nodes[2][:], dst_f[:, edges_of(2)])
-        nc.scalar.dma_start(dst_nodes[3][:], dst_f[:, edges_of(3)])
+        nc.sync.dma_start(dst_weights[:], w_dst)
+        for piece in range(PIECES):
+            nc.sync.dma_start(dst_nodes[piece][:], dst_f[:, edges_of(piece)])
         nc.sync.dma_start(offsets[:], offs)
-        nc.scalar.dma_start(src_weights[:], w_src)
+        nc.sync.dma_start(src_weights[:], w_src)
         nc.sync.dma_start(nodes[:], table)
 
         for piece in range(PIECES):

@@ -24,21 +24,20 @@ def tile_h_h_edgeapplymoudle_kernel(tc, table, w_src, w_dst, dst_f, offs, out):
         nodes = held.tile([P, NODES], BF16, name="nodes")
         src_weights = held.tile([P, P], BF16, name="src_weights")
         dst_weights = held.tile([P, P], BF16, name="dst_weights")
-        dst_nodes = [held.tile([P, PIECE], BF16, name=f"dst_nodes{piece}") for piece in range(PIECES)]
+        dst_nodes = held.tile([P, EDGES], BF16, name="dst_nodes")
         banks = [psum.tile([P, PIECE], F32, name=f"bank{piece}") for piece in range(PIECES)]
 
         def edges_of(piece):
             return slice(piece * PIECE, (piece + 1) * PIECE)
 
         nc.sync.dma_start(dst_weights[:], w_dst)
-        for piece in range(PIECES):
-            nc.sync.dma_start(dst_nodes[piece][:], dst_f[:, edges_of(piece)])
+        nc.sync.dma_start(dst_nodes[:], dst_f)
         nc.sync.dma_start(offsets[:], offs)
         nc.sync.dma_start(src_weights[:], w_src)
         nc.sync.dma_start(nodes[:], table)
 
         for piece in range(PIECES):
-            nc.tensor.matmul(banks[piece][:], dst_weights[:], dst_nodes[piece][:], start=True, stop=False)
+            nc.tensor.matmul(banks[piece][:], dst_weights[:], dst_nodes[:, edges_of(piece)], start=True, stop=False)
 
         for piece in range(PIECES):
             entries = slice(piece * PIECE // PER_COLUMN, (piece + 1) * PIECE // PER_COLUMN)

@@ -30,10 +30,10 @@ def tile_h_h_edgeapplymoudle_kernel(tc, table, w_src, w_dst, dst_f, offs, out):
         def edges_of(piece):
             return slice(piece * PIECE, (piece + 1) * PIECE)
 
-        nc.sync.dma_start(dst_weights[:], w_dst)
         nc.sync.dma_start(dst_nodes[:], dst_f)
+        nc.scalar.dma_start(dst_weights[:], w_dst)
         nc.sync.dma_start(offsets[:], offs)
-        nc.sync.dma_start(src_weights[:], w_src)
+        nc.scalar.dma_start(src_weights[:], w_src)
         nc.sync.dma_start(nodes[:], table)
 
         for piece in range(PIECES):

import concourse.mybir as mybir

BF16, F32, U16 = mybir.dt.bfloat16, mybir.dt.float32, mybir.dt.uint16
SIGMOID = mybir.ActivationFunctionType.Sigmoid

P = 128
NODES = 512
EDGES = 1024
PER_COLUMN = 16

FLOPS = 2 * (2 * P) * P * EDGES

PIECE = 256
PIECES = EDGES // PIECE


def tile_h_h_edgeapplymoudle_kernel(tc, table, w_src, w_dst, dst_f, offs, out):
    nc = tc.nc
    with (
        tc.tile_pool(name="held", bufs=1) as held,
        tc.psum_pool(name="psum", bufs=1) as psum,
    ):
        offsets = held.tile([P, EDGES // PER_COLUMN], U16, name="offsets")
        nodes = held.tile([P, NODES], BF16, name="nodes")
        src_weights = held.tile([P, P], BF16, name="src_weights")
        dst_weights = held.tile([P, P], BF16, name="dst_weights")
        dst_nodes = held.tile([P, EDGES], BF16, name="dst_nodes")
        banks = [psum.tile([P, PIECE], F32, name=f"bank{piece}") for piece in range(PIECES)]

        def edges_of(piece):
            return slice(piece * PIECE, (piece + 1) * PIECE)

        nc.sync.dma_start(dst_nodes[:], dst_f)
        nc.scalar.dma_start(dst_weights[:], w_dst)
        nc.sync.dma_start(offsets[:], offs)
        nc.scalar.dma_start(src_weights[:], w_src)
        nc.sync.dma_start(nodes[:], table)

        for piece in range(PIECES):
            nc.tensor.matmul(banks[piece][:], dst_weights[:], dst_nodes[:, edges_of(piece)], start=True, stop=False)

        for piece in range(PIECES):
            entries = slice(piece * PIECE // PER_COLUMN, (piece + 1) * PIECE // PER_COLUMN)
            gated = held.tile([P, PIECE], F32, name=f"gated{piece}")
            nc.tensor.matmul(banks[piece][:], src_weights[:], nodes[:].indirect(offsets[:, entries]), start=False, stop=True)
            nc.scalar.activation(gated[:], banks[piece][:], SIGMOID)
            store_queue = nc.sync if piece < PIECES - 1 else nc.scalar
            store_queue.dma_start(out[:, edges_of(piece)], gated[:])
